import numpy as np
import ml_dtypes


def mxq(x, axis, fmt="e4m3"):
    dtype, down = {"e4m3": (ml_dtypes.float8_e4m3fn, 7), "e5m2": (ml_dtypes.float8_e5m2, 14)}[fmt]
    v = np.moveaxis(np.asarray(x, np.float32).astype(ml_dtypes.bfloat16).astype(np.float64), axis, -1)
    blocks = v.reshape(v.shape[:-1] + (-1, 32))
    amax = np.abs(blocks).max(-1, keepdims=True)
    byte = np.maximum(np.where(amax > 0, np.frexp(amax)[1] - 1 + 127, 0) - down, 1)
    scale = np.exp2(byte - 127.0)
    codes = (blocks / scale).astype(np.float32).astype(dtype).astype(np.float64)
    return np.moveaxis((codes * scale).reshape(v.shape), -1, axis)


WIDE = False


def mx_kscale(k):
    if not WIDE:
        return np.ones(k)
    levels = np.array([10, -10, 5, -5, 0])
    a = np.random.permutation(np.resize(levels, k // 512 * 4)).reshape(k // 512, 4)
    idx = np.arange(k)
    return np.exp2(a[idx // 512, idx % 128 // 32])


BF16 = ml_dtypes.bfloat16


def bf(x):
    return np.asarray(x, np.float32).astype(BF16)


def f64(x):
    return np.asarray(x).astype(np.float64)


E2M1 = np.array([0.0, 0.5, 1.0, 1.5, 2.0, 3.0, 4.0, 6.0, -0.0, -0.5, -1.0, -1.5, -2.0, -3.0, -4.0, -6.0])


def pack_weight(w, fmt):
    k, n = w.shape
    w = f64(bf(w)).reshape(k // 32, 32, n)
    amax = np.abs(w).max(1)
    if fmt == "e4m3":
        byte = np.frexp(amax)[1] - 1 + 127 - 7
    else:
        mant, ex = np.frexp(amax / 6.0)
        byte = np.where(mant > 0.5, ex, ex - 1) + 127
    byte = np.clip(np.where(amax > 0, byte, 1), 1, 254)
    scaled = (w * np.exp2(127.0 - byte)[:, None, :]).reshape(k, n).astype(np.float32)
    by_word = np.ascontiguousarray(scaled.reshape(k // 512, 128, 4, n).transpose(0, 1, 3, 2))
    if fmt == "e4m3":
        words = by_word.astype(ml_dtypes.float8_e4m3fn).view(np.uint8)
    else:
        c = by_word.astype(ml_dtypes.float4_e2m1fn).view(np.uint8) & 0xF
        words = c[..., 0::2] | (c[..., 1::2] << 4)
    return np.ascontiguousarray(words), np.ascontiguousarray(byte.astype(np.uint8).reshape(k // 512, 16, n))


def unpack_weight(words, scales, fmt):
    g, p, n, _ = words.shape
    if fmt == "e4m3":
        vals = np.ascontiguousarray(words).view(ml_dtypes.float8_e4m3fn).astype(np.float64)
    else:
        nib = np.empty((g, p, n, 4), np.uint8)
        nib[..., 0::2] = words & 0xF
        nib[..., 1::2] = words >> 4
        vals = E2M1[nib]
    vals = vals * np.repeat(np.exp2(scales.astype(np.float64) - 127.0), 8, axis=1)[..., None]
    return vals.transpose(0, 1, 3, 2).reshape(g * 512, n)

def pack4(w):
    words, scales = pack_weight(w, "e2m1")
    return words.reshape(words.shape[0], 128, -1), scales


def unpack4(words, scales):
    return unpack_weight(words.reshape(words.shape[0], 128, -1, 2), scales, "e2m1")


B, C, D, T, H, W, P = 1, 1024, 512, 8, 16, 16, 2
N = T * H * W
NP = T * (H // P) * (W // P)


def conv1x1(wq, b, xq):
    return ((wq @ xq) + b[None, :, None]).reshape(B, D, T, H, W)


def maxpool(v):
    return v.reshape(B, D, T, H // P, P, W // P, P).max(axis=(4, 6))


def setup_inputs():
    s = mx_kscale(C)
    a = 1.0 / np.sqrt(C) / s[None, :]
    x = bf(np.random.standard_normal((B, C, T, H, W)) * s[None, :, None, None, None])
    g_w_words, g_w_scales = pack4(np.ascontiguousarray((np.random.standard_normal((D, C)) * 0.15 * a).T))
    g_b = bf(np.random.standard_normal(D) * 0.03)
    theta_w_words, theta_w_scales = pack4(np.ascontiguousarray((np.random.standard_normal((D, C)) * 2.0 * a).T))
    theta_b = bf(np.random.standard_normal(D) * 0.2)
    phi_w_words, phi_w_scales = pack4(np.ascontiguousarray((np.random.standard_normal((D, C)) * a).T))
    phi_b = bf(np.random.standard_normal(D) * 0.1)
    return {"x": x,
            "g_w_words": g_w_words,
            "g_w_scales": g_w_scales,
            "g_b": g_b,
            "theta_w_words": theta_w_words,
            "theta_w_scales": theta_w_scales,
            "theta_b": theta_b,
            "phi_w_words": phi_w_words,
            "phi_w_scales": phi_w_scales,
            "phi_b": phi_b}


def reference(x, g_w_words, g_w_scales, g_b, theta_w_words, theta_w_scales, theta_b, phi_w_words, phi_w_scales, phi_b):
    xq = mxq(f64(x).reshape(B, C, N), 1, "e4m3")
    g_x = maxpool(conv1x1(unpack4(g_w_words, g_w_scales).T, f64(g_b), xq)).reshape(B, D, NP)
    theta_x = conv1x1(unpack4(theta_w_words, theta_w_scales).T, f64(theta_b), xq).reshape(B, D, N)
    phi_x = maxpool(conv1x1(unpack4(phi_w_words, phi_w_scales).T, f64(phi_b), xq)).reshape(B, D, NP)
    return g_x, theta_x, phi_x

@@ -1,0 +1,213 @@
+from contextlib import ExitStack
+
+import concourse.mybir as mybir
+from concourse.masks import make_identity
+
+F32 = mybir.dt.float32
+BF16 = mybir.dt.bfloat16
+I32 = mybir.dt.int32
+U32 = mybir.dt.uint32
+U8 = mybir.dt.uint8
+FP8X4 = mybir.dt.float8_e4m3fn_x4
+FP4X4 = mybir.dt.float4_e2m1fn_x4
+
+P = 128
+PACK = 4
+K_PASS = P * PACK
+CHANNELS = 1024
+GROUPS = CHANNELS // K_PASS
+D = 512
+D_TILES = D // P
+FRAMES = 8
+HEIGHT = 16
+WIDTH = 16
+POSITIONS = FRAMES * HEIGHT * WIDTH
+CHUNK = 512
+CHUNKS = POSITIONS // CHUNK
+WINDOW = 2
+POOLED = CHUNK // (WINDOW * WINDOW)
+PSUM_BANKS = 8
+RUN = 4
+
+G = 0
+THETA = 1
+PHI = 2
+CONVS = 3
+
+HEAD_VECTOR_COLS = 352
+STEADY_VECTOR_COLS = 128
+
+FLOPS = 2 * CONVS * D * CHANNELS * POSITIONS
+
+
+def tile_nonlocalblocknd_pa_kernel(
+    tc,
+    x,
+    g_w_words,
+    g_w_scales,
+    g_b,
+    theta_w_words,
+    theta_w_scales,
+    theta_b,
+    phi_w_words,
+    phi_w_scales,
+    phi_b,
+    out_0,
+    out_1,
+    out_2,
+):
+    nc = tc.nc
+    dram_words = (g_w_words, theta_w_words, phi_w_words)
+    dram_scales = (g_w_scales, theta_w_scales, phi_w_scales)
+    dram_bias = (g_b, theta_b, phi_b)
+    dram_out = [o[0].rearrange("(d p) n -> p d n", p=P) for o in (out_0, out_1, out_2)]
+    x_rows = x[0].rearrange("(g p t) f h w -> g p t (f h w)", g=GROUPS, p=P, t=PACK)
+
+    with ExitStack() as ctx:
+        keep = ctx.enter_context(tc.tile_pool(name="keep", bufs=1))
+        stage = ctx.enter_context(tc.tile_pool(name="stage", bufs=4))
+        results = ctx.enter_context(tc.tile_pool(name="results", bufs=6))
+        psum = ctx.enter_context(tc.psum_pool(name="psum", bufs=PSUM_BANKS))
+        ctx.enter_context(tc.manual_schedule())
+
+        raw = {}
+        x_codes = {}
+        x_scales = {}
+        for j in range(CHUNKS):
+            for g in range(GROUPS):
+                raw[(j, g)] = keep.tile([P, PACK, CHUNK], BF16, name="raw_%d_%d" % (j, g))
+                x_codes[(j, g)] = keep.tile(
+                    [P, CHUNK], U32, name="x_codes_%d_%d" % (j, g), align_bytes=64
+                )
+                x_scales[(j, g)] = keep.tile(
+                    [P, CHUNK], U8, name="x_scales_%d_%d" % (j, g), align_bytes=64
+                )
+        w_words = []
+        w_scales = []
+        for c in range(CONVS):
+            w_words.append(keep.tile([P, GROUPS, 2 * D], U8, name="w_words_%d" % c, align_bytes=64))
+            w_scales.append(keep.tile([P, GROUPS, D], U8, name="w_scales_%d" % c, align_bytes=64))
+        bias_rows = keep.tile([P, P], BF16, name="bias_rows")
+        identity = keep.tile([P, P], BF16, name="identity")
+        bias = keep.tile([P, CONVS * D_TILES], F32, name="bias")
+
+        def load_x(j, g):
+            nc.sync.dma_start(
+                out=raw[(j, g)][:], in_=x_rows[g, :, :, j * CHUNK : (j + 1) * CHUNK]
+            )
+
+        def load_weight(c):
+            for r in range(4):
+                nc.sync.dma_start(
+                    out=w_scales[c][r:P:32, :, :].bitcast(I32),
+                    in_=dram_scales[c][:, r:16:4, :].rearrange("g q n -> q g n").bitcast(I32),
+                )
+            nc.sync.dma_start(
+                out=w_words[c][:].bitcast(I32),
+                in_=dram_words[c].rearrange("g p b -> p g b").bitcast(I32),
+            )
+
+        for c in range(CONVS):
+            nc.vector.memset(w_scales[c][:].rearrange("p g n -> p (g n)").bitcast(I32), 0)
+
+        nc.gpsimd.memset(bias_rows[:], 0.0)
+        for c in range(CONVS):
+            nc.gpsimd.dma_start(
+                out=bias_rows[c * D_TILES : (c + 1) * D_TILES, :],
+                in_=dram_bias[c].rearrange("(d n) -> d n", n=P),
+            )
+        make_identity(nc, identity[:])
+
+        load_x(0, 0)
+        load_weight(G)
+        load_x(0, 1)
+        load_weight(THETA)
+        load_x(1, 0)
+        load_x(1, 1)
+        load_weight(PHI)
+        for j in range(2, CHUNKS):
+            for g in range(GROUPS):
+                load_x(j, g)
+
+        bias_cols = psum.tile([P, P], BF16, name="bias_cols", tag="acc")
+        nc.tensor.transpose(bias_cols[:], bias_rows[:], identity[:])
+
+        def regroup(j, g, vector_cols):
+            grouped = stage.tile([P, CHUNK, PACK], BF16, name="grouped", align_bytes=64)
+            src = raw[(j, g)][:].rearrange("p t (n i) -> p n t i", i=RUN)
+            dst = grouped[:].rearrange("p (n i) t -> p n t i", i=RUN)
+            split = (CHUNK - vector_cols) // RUN
+            nc.scalar.copy(out=dst[:, :split], in_=src[:, :split])
+            nc.vector.tensor_copy(out=dst[:, split:], in_=src[:, split:])
+            return grouped
+
+        def quantise(j, g, grouped):
+            nc.vector.quantize_mx(
+                out=x_codes[(j, g)][:].bitcast(FP8X4),
+                scales=x_scales[(j, g)][:],
+                in_=grouped[:].rearrange("p n t -> p (n t)"),
+            )
+
+        def multiply(j, c):
+            banks = [psum.tile([P, CHUNK], F32, name="acc", tag="acc") for d in range(D_TILES)]
+            for g in range(GROUPS):
+                for d in range(D_TILES):
+                    nc.tensor.matmul_mx(
+                        out=banks[d][:],
+                        lhsT=w_words[c][:, g, 2 * P * d : 2 * P * (d + 1)].bitcast(FP4X4),
+                        lhsT_scale=w_scales[c][:, g, P * d : P * (d + 1)],
+                        rhs=x_codes[(j, g)][:].bitcast(FP8X4),
+                        rhs_scale=x_scales[(j, g)][:],
+                        start=(g == 0),
+                        stop=(g == GROUPS - 1),
+                    )
+            return banks
+
+        def store_plain(j, c, banks):
+            for d in range(D_TILES):
+                plain = results.tile([P, CHUNK], F32, name="plain")
+                nc.scalar.activation(
+                    out=plain[:],
+                    in_=banks[d][:],
+                    func=mybir.ActivationFunctionType.Identity,
+                    bias=bias[:, c * D_TILES + d : c * D_TILES + d + 1],
+                )
+                nc.sync.dma_start(
+                    out=dram_out[c][:, d, j * CHUNK : (j + 1) * CHUNK], in_=plain[:]
+                )
+
+        def store_pooled(j, c, banks):
+            pooled = results.tile([P, D_TILES, POOLED], F32, name="pooled")
+            for d in range(D_TILES):
+                nc.vector.tensor_reduce(
+                    out=pooled[:, d, :].rearrange("p (a w) -> p a w", w=WIDTH // WINDOW),
+                    in_=banks[d][:].rearrange(
+                        "p (a u w v) -> p a w u v", u=WINDOW, w=WIDTH // WINDOW, v=WINDOW
+                    ),
+                    axis=mybir.AxisListType.XY,
+                    op=mybir.AluOpType.max,
+                )
+                nc.gpsimd.tensor_scalar(
+                    out=pooled[:, d, :],
+                    in0=pooled[:, d, :],
+                    scalar1=1.0,
+                    scalar2=bias[:, c * D_TILES + d : c * D_TILES + d + 1],
+                    op0=mybir.AluOpType.mult,
+                    op1=mybir.AluOpType.add,
+                )
+            nc.sync.dma_start(
+                out=dram_out[c][:, :, j * POOLED : (j + 1) * POOLED], in_=pooled[:]
+            )
+
+        for g in range(GROUPS):
+            quantise(0, g, regroup(0, g, HEAD_VECTOR_COLS))
+        nc.vector.tensor_copy(out=bias[:], in_=bias_cols[:, : CONVS * D_TILES])
+
+        for j in range(CHUNKS):
+            store_pooled(j, G, multiply(j, G))
+            if j + 1 < CHUNKS:
+                halves = [regroup(j + 1, g, STEADY_VECTOR_COLS) for g in range(GROUPS)]
+                for g in range(GROUPS):
+                    quantise(j + 1, g, halves[g])
+            store_plain(j, THETA, multiply(j, THETA))
+            store_pooled(j, PHI, multiply(j, PHI))

@@ -129,9 +129,6 @@ def tile_nonlocalblocknd_pa_kernel(
             for g in range(GROUPS):
                 load_x(j, g)
 
-        bias_cols = psum.tile([P, P], BF16, name="bias_cols", tag="acc")
-        nc.tensor.transpose(bias_cols[:], bias_rows[:], identity[:])
-
         def regroup(j, g, vector_cols):
             grouped = stage.tile([P, CHUNK, PACK], BF16, name="grouped", align_bytes=64)
             src = raw[(j, g)][:].rearrange("p t (n i) -> p n t i", i=RUN)
@@ -163,15 +160,30 @@ def tile_nonlocalblocknd_pa_kernel(
                     )
             return banks
 
-        def store_plain(j, c, banks):
+        def spread_bias():
+            bias_cols = psum.tile([P, P], BF16, name="bias_cols", tag="acc")
+            nc.tensor.transpose(bias_cols[:], bias_rows[:], identity[:])
+            nc.vector.tensor_copy(out=bias[:], in_=bias_cols[:, : CONVS * D_TILES])
+
+        def store_plain(j, c, banks, vector_helps):
             for d in range(D_TILES):
                 plain = results.tile([P, CHUNK], F32, name="plain")
-                nc.scalar.activation(
-                    out=plain[:],
-                    in_=banks[d][:],
-                    func=mybir.ActivationFunctionType.Identity,
-                    bias=bias[:, c * D_TILES + d : c * D_TILES + d + 1],
-                )
+                bias_d = bias[:, c * D_TILES + d : c * D_TILES + d + 1]
+                if vector_helps and d % 2 == 1:
+                    nc.vector.tensor_scalar(
+                        out=plain[:],
+                        in0=banks[d][:],
+                        scalar1=bias_d,
+                        scalar2=None,
+                        op0=mybir.AluOpType.add,
+                    )
+                else:
+                    nc.scalar.activation(
+                        out=plain[:],
+                        in_=banks[d][:],
+                        func=mybir.ActivationFunctionType.Identity,
+                        bias=bias_d,
+                    )
                 nc.sync.dma_start(
                     out=dram_out[c][:, d, j * CHUNK : (j + 1) * CHUNK], in_=plain[:]
                 )
@@ -201,13 +213,19 @@ def tile_nonlocalblocknd_pa_kernel(
 
         for g in range(GROUPS):
             quantise(0, g, regroup(0, g, HEAD_VECTOR_COLS))
-        nc.vector.tensor_copy(out=bias[:], in_=bias_cols[:, : CONVS * D_TILES])
 
-        for j in range(CHUNKS):
-            store_pooled(j, G, multiply(j, G))
-            if j + 1 < CHUNKS:
-                halves = [regroup(j + 1, g, STEADY_VECTOR_COLS) for g in range(GROUPS)]
-                for g in range(GROUPS):
-                    quantise(j + 1, g, halves[g])
-            store_plain(j, THETA, multiply(j, THETA))
+        for j in range(CHUNKS - 1):
+            banks = multiply(j, G)
+            if j == 0:
+                spread_bias()
+            store_pooled(j, G, banks)
+            halves = [regroup(j + 1, g, STEADY_VECTOR_COLS) for g in range(GROUPS)]
+            for g in range(GROUPS):
+                quantise(j + 1, g, halves[g])
+            store_plain(j, THETA, multiply(j, THETA), False)
             store_pooled(j, PHI, multiply(j, PHI))
+
+        j = CHUNKS - 1
+        store_pooled(j, G, multiply(j, G))
+        store_pooled(j, PHI, multiply(j, PHI))
+        store_plain(j, THETA, multiply(j, THETA), True)

@@ -27,6 +27,7 @@ CHUNKS = POSITIONS // CHUNK
 WINDOW = 2
 POOLED = CHUNK // (WINDOW * WINDOW)
 PSUM_BANKS = 8
+RESULT_BUFS = 16
 RUN = 4
 
 G = 0
@@ -66,7 +67,7 @@ def tile_nonlocalblocknd_pa_kernel(
     with ExitStack() as ctx:
         keep = ctx.enter_context(tc.tile_pool(name="keep", bufs=1))
         stage = ctx.enter_context(tc.tile_pool(name="stage", bufs=4))
-        results = ctx.enter_context(tc.tile_pool(name="results", bufs=6))
+        results = ctx.enter_context(tc.tile_pool(name="results", bufs=RESULT_BUFS))
         psum = ctx.enter_context(tc.psum_pool(name="psum", bufs=PSUM_BANKS))
         ctx.enter_context(tc.manual_schedule())
 
@@ -145,19 +146,22 @@ def tile_nonlocalblocknd_pa_kernel(
                 in_=grouped[:].rearrange("p n t -> p (n t)"),
             )
 
-        def multiply(j, c):
+        def multiply(j, c, group_by_group=False):
             banks = [psum.tile([P, CHUNK], F32, name="acc", tag="acc") for d in range(D_TILES)]
-            for g in range(GROUPS):
-                for d in range(D_TILES):
-                    nc.tensor.matmul_mx(
-                        out=banks[d][:],
-                        lhsT=w_words[c][:, g, 2 * P * d : 2 * P * (d + 1)].bitcast(FP4X4),
-                        lhsT_scale=w_scales[c][:, g, P * d : P * (d + 1)],
-                        rhs=x_codes[(j, g)][:].bitcast(FP8X4),
-                        rhs_scale=x_scales[(j, g)][:],
-                        start=(g == 0),
-                        stop=(g == GROUPS - 1),
-                    )
+            if group_by_group:
+                passes = [(g, d) for g in range(GROUPS) for d in range(D_TILES)]
+            else:
+                passes = [(g, d) for d in range(D_TILES) for g in range(GROUPS)]
+            for g, d in passes:
+                nc.tensor.matmul_mx(
+                    out=banks[d][:],
+                    lhsT=w_words[c][:, g, 2 * P * d : 2 * P * (d + 1)].bitcast(FP4X4),
+                    lhsT_scale=w_scales[c][:, g, P * d : P * (d + 1)],
+                    rhs=x_codes[(j, g)][:].bitcast(FP8X4),
+                    rhs_scale=x_scales[(j, g)][:],
+                    start=(g == 0),
+                    stop=(g == GROUPS - 1),
+                )
             return banks
 
         def spread_bias():
@@ -165,34 +169,24 @@ def tile_nonlocalblocknd_pa_kernel(
             nc.tensor.transpose(bias_cols[:], bias_rows[:], identity[:])
             nc.vector.tensor_copy(out=bias[:], in_=bias_cols[:, : CONVS * D_TILES])
 
-        def store_plain(j, c, banks, vector_helps):
+        def store_plain(j, c, banks):
             for d in range(D_TILES):
                 plain = results.tile([P, CHUNK], F32, name="plain")
-                bias_d = bias[:, c * D_TILES + d : c * D_TILES + d + 1]
-                if vector_helps and d % 2 == 1:
-                    nc.vector.tensor_scalar(
-                        out=plain[:],
-                        in0=banks[d][:],
-                        scalar1=bias_d,
-                        scalar2=None,
-                        op0=mybir.AluOpType.add,
-                    )
-                else:
-                    nc.scalar.activation(
-                        out=plain[:],
-                        in_=banks[d][:],
-                        func=mybir.ActivationFunctionType.Identity,
-                        bias=bias_d,
-                    )
+                nc.scalar.activation(
+                    out=plain[:],
+                    in_=banks[d][:],
+                    func=mybir.ActivationFunctionType.Identity,
+                    bias=bias[:, c * D_TILES + d : c * D_TILES + d + 1],
+                )
                 nc.sync.dma_start(
                     out=dram_out[c][:, d, j * CHUNK : (j + 1) * CHUNK], in_=plain[:]
                 )
 
         def store_pooled(j, c, banks):
-            pooled = results.tile([P, D_TILES, POOLED], F32, name="pooled")
             for d in range(D_TILES):
+                pooled = results.tile([P, POOLED], F32, name="pooled")
                 nc.vector.tensor_reduce(
-                    out=pooled[:, d, :].rearrange("p (a w) -> p a w", w=WIDTH // WINDOW),
+                    out=pooled[:].rearrange("p (a w) -> p a w", w=WIDTH // WINDOW),
                     in_=banks[d][:].rearrange(
                         "p (a u w v) -> p a w u v", u=WINDOW, w=WIDTH // WINDOW, v=WINDOW
                     ),
@@ -200,32 +194,28 @@ def tile_nonlocalblocknd_pa_kernel(
                     op=mybir.AluOpType.max,
                 )
                 nc.gpsimd.tensor_scalar(
-                    out=pooled[:, d, :],
-                    in0=pooled[:, d, :],
+                    out=pooled[:],
+                    in0=pooled[:],
                     scalar1=1.0,
                     scalar2=bias[:, c * D_TILES + d : c * D_TILES + d + 1],
                     op0=mybir.AluOpType.mult,
                     op1=mybir.AluOpType.add,
                 )
-            nc.sync.dma_start(
-                out=dram_out[c][:, :, j * POOLED : (j + 1) * POOLED], in_=pooled[:]
-            )
+                nc.sync.dma_start(
+                    out=dram_out[c][:, d, j * POOLED : (j + 1) * POOLED], in_=pooled[:]
+                )
 
         for g in range(GROUPS):
             quantise(0, g, regroup(0, g, HEAD_VECTOR_COLS))
 
-        for j in range(CHUNKS - 1):
-            banks = multiply(j, G)
+        for j in range(CHUNKS):
+            banks = multiply(j, G, group_by_group=(j == 0))
             if j == 0:
                 spread_bias()
             store_pooled(j, G, banks)
-            halves = [regroup(j + 1, g, STEADY_VECTOR_COLS) for g in range(GROUPS)]
-            for g in range(GROUPS):
-                quantise(j + 1, g, halves[g])
-            store_plain(j, THETA, multiply(j, THETA), False)
+            if j + 1 < CHUNKS:
+                halves = [regroup(j + 1, g, STEADY_VECTOR_COLS) for g in range(GROUPS)]
+                for g in range(GROUPS):
+                    quantise(j + 1, g, halves[g])
+            store_plain(j, THETA, multiply(j, THETA))
             store_pooled(j, PHI, multiply(j, PHI))
-
-        j = CHUNKS - 1
-        store_pooled(j, G, multiply(j, G))
-        store_pooled(j, PHI, multiply(j, PHI))
-        store_plain(j, THETA, multiply(j, THETA), True)

@@ -38,6 +38,9 @@ CONVS = 3
 HEAD_VECTOR_COLS = 352
 STEADY_VECTOR_COLS = 128
 
+WARM_ZEROS = 5
+WARM_RAW = 3
+
 FLOPS = 2 * CONVS * D * CHANNELS * POSITIONS
 
 
@@ -91,6 +94,7 @@ def tile_nonlocalblocknd_pa_kernel(
         bias_rows = keep.tile([P, P], BF16, name="bias_rows")
         identity = keep.tile([P, P], BF16, name="identity")
         bias = keep.tile([P, CONVS * D_TILES], F32, name="bias")
+        zeros = keep.tile([P, CHUNK], BF16, name="zeros")
 
         def load_x(j, g):
             nc.sync.dma_start(
@@ -108,7 +112,9 @@ def tile_nonlocalblocknd_pa_kernel(
                 in_=dram_words[c].rearrange("g p b -> p g b").bitcast(I32),
             )
 
-        for c in range(CONVS):
+        nc.vector.memset(w_scales[G][:].rearrange("p g n -> p (g n)").bitcast(I32), 0)
+        nc.vector.memset(zeros[:], 0.0)
+        for c in (THETA, PHI):
             nc.vector.memset(w_scales[c][:].rearrange("p g n -> p (g n)").bitcast(I32), 0)
 
         nc.gpsimd.memset(bias_rows[:], 0.0)
@@ -204,6 +210,15 @@ def tile_nonlocalblocknd_pa_kernel(
                 nc.sync.dma_start(
                     out=dram_out[c][:, d, j * POOLED : (j + 1) * POOLED], in_=pooled[:]
                 )
+
+        def idle_matmul(operand):
+            unused = psum.tile([P, CHUNK], F32, name="unused", tag="acc")
+            nc.tensor.matmul(unused[:], lhsT=operand[:, :P], rhs=operand, start=True, stop=True)
+
+        for i in range(WARM_ZEROS):
+            idle_matmul(zeros[:])
+        for i in range(WARM_RAW):
+            idle_matmul(raw[(0, 0)][:, 0, :])
 
         for g in range(GROUPS):
             quantise(0, g, regroup(0, g, HEAD_VECTOR_COLS))

@@ -1,7 +1,6 @@
 from contextlib import ExitStack
 
 import concourse.mybir as mybir
-from concourse.masks import make_identity
 
 F32 = mybir.dt.float32
 BF16 = mybir.dt.bfloat16
@@ -91,9 +90,9 @@ def tile_nonlocalblocknd_pa_kernel(
         for c in range(CONVS):
             w_words.append(keep.tile([P, GROUPS, 2 * D], U8, name="w_words_%d" % c, align_bytes=64))
             w_scales.append(keep.tile([P, GROUPS, D], U8, name="w_scales_%d" % c, align_bytes=64))
-        bias_rows = keep.tile([P, P], BF16, name="bias_rows")
-        identity = keep.tile([P, P], BF16, name="identity")
-        bias = keep.tile([P, CONVS * D_TILES], F32, name="bias")
+        bias_words = []
+        for c in range(CONVS):
+            bias_words.append(keep.tile([P, D_TILES, 2], BF16, name="bias_words_%d" % c))
         zeros = keep.tile([P, CHUNK], BF16, name="zeros")
 
         def load_x(j, g):
@@ -117,13 +116,15 @@ def tile_nonlocalblocknd_pa_kernel(
         for c in (THETA, PHI):
             nc.vector.memset(w_scales[c][:].rearrange("p g n -> p (g n)").bitcast(I32), 0)
 
-        nc.gpsimd.memset(bias_rows[:], 0.0)
-        for c in range(CONVS):
-            nc.gpsimd.dma_start(
-                out=bias_rows[c * D_TILES : (c + 1) * D_TILES, :],
-                in_=dram_bias[c].rearrange("(d n) -> d n", n=P),
-            )
-        make_identity(nc, identity[:])
+        with nc.allow_non_contiguous_dma(reason="one bias value to a partition"):
+            for c in range(CONVS):
+                nc.gpsimd.dma_start(
+                    out=bias_words[c][:, :, 0:1],
+                    in_=dram_bias[c].rearrange("(d p o) -> p d o", p=P, o=1),
+                )
+
+        def bias_of(c, d):
+            return bias_words[c][:, d, 0:1]
 
         load_x(0, 0)
         load_weight(G)
@@ -170,11 +171,6 @@ def tile_nonlocalblocknd_pa_kernel(
                 )
             return banks
 
-        def spread_bias():
-            bias_cols = psum.tile([P, P], BF16, name="bias_cols", tag="acc")
-            nc.tensor.transpose(bias_cols[:], bias_rows[:], identity[:])
-            nc.vector.tensor_copy(out=bias[:], in_=bias_cols[:, : CONVS * D_TILES])
-
         def store_plain(j, c, banks):
             for d in range(D_TILES):
                 plain = results.tile([P, CHUNK], F32, name="plain")
@@ -182,7 +178,7 @@ def tile_nonlocalblocknd_pa_kernel(
                     out=plain[:],
                     in_=banks[d][:],
                     func=mybir.ActivationFunctionType.Identity,
-                    bias=bias[:, c * D_TILES + d : c * D_TILES + d + 1],
+                    bias=bias_of(c, d),
                 )
                 nc.sync.dma_start(
                     out=dram_out[c][:, d, j * CHUNK : (j + 1) * CHUNK], in_=plain[:]
@@ -203,7 +199,7 @@ def tile_nonlocalblocknd_pa_kernel(
                     out=pooled[:],
                     in0=pooled[:],
                     scalar1=1.0,
-                    scalar2=bias[:, c * D_TILES + d : c * D_TILES + d + 1],
+                    scalar2=bias_of(c, d),
                     op0=mybir.AluOpType.mult,
                     op1=mybir.AluOpType.add,
                 )
@@ -225,8 +221,6 @@ def tile_nonlocalblocknd_pa_kernel(
 
         for j in range(CHUNKS):
             banks = multiply(j, G, group_by_group=(j == 0))
-            if j == 0:
-                spread_bias()
             store_pooled(j, G, banks)
             if j + 1 < CHUNKS:
                 halves = [regroup(j + 1, g, STEADY_VECTOR_COLS) for g in range(GROUPS)]

@@ -153,22 +153,33 @@ def tile_nonlocalblocknd_pa_kernel(
                 in_=grouped[:].rearrange("p n t -> p (n t)"),
             )
 
-        def multiply(j, c, group_by_group=False):
-            banks = [psum.tile([P, CHUNK], F32, name="acc", tag="acc") for d in range(D_TILES)]
-            if group_by_group:
-                passes = [(g, d) for g in range(GROUPS) for d in range(D_TILES)]
-            else:
-                passes = [(g, d) for d in range(D_TILES) for g in range(GROUPS)]
-            for g, d in passes:
-                nc.tensor.matmul_mx(
-                    out=banks[d][:],
-                    lhsT=w_words[c][:, g, 2 * P * d : 2 * P * (d + 1)].bitcast(FP4X4),
-                    lhsT_scale=w_scales[c][:, g, P * d : P * (d + 1)],
-                    rhs=x_codes[(j, g)][:].bitcast(FP8X4),
-                    rhs_scale=x_scales[(j, g)][:],
-                    start=(g == 0),
-                    stop=(g == GROUPS - 1),
-                )
+        def four_banks():
+            return [psum.tile([P, CHUNK], F32, name="acc", tag="acc") for d in range(D_TILES)]
+
+        def one_pass(j, c, d, g, bank):
+            nc.tensor.matmul_mx(
+                out=bank[:],
+                lhsT=w_words[c][:, g, 2 * P * d : 2 * P * (d + 1)].bitcast(FP4X4),
+                lhsT_scale=w_scales[c][:, g, P * d : P * (d + 1)],
+                rhs=x_codes[(j, g)][:].bitcast(FP8X4),
+                rhs_scale=x_scales[(j, g)][:],
+                start=(g == 0),
+                stop=(g == GROUPS - 1),
+            )
+
+        def multiply(j, c):
+            banks = four_banks()
+            for d in range(D_TILES):
+                for g in range(GROUPS):
+                    one_pass(j, c, d, g, banks[d])
+            return banks
+
+        def multiply_first_two():
+            banks = {G: four_banks(), THETA: four_banks()}
+            for g in range(GROUPS):
+                for c in (G, THETA):
+                    for d in range(D_TILES):
+                        one_pass(0, c, d, g, banks[c][d])
             return banks
 
         def store_plain(j, c, banks):
@@ -220,11 +231,11 @@ def tile_nonlocalblocknd_pa_kernel(
             quantise(0, g, regroup(0, g, HEAD_VECTOR_COLS))
 
         for j in range(CHUNKS):
-            banks = multiply(j, G, group_by_group=(j == 0))
-            store_pooled(j, G, banks)
+            first_two = multiply_first_two() if j == 0 else {}
+            store_pooled(j, G, first_two[G] if j == 0 else multiply(j, G))
             if j + 1 < CHUNKS:
                 halves = [regroup(j + 1, g, STEADY_VECTOR_COLS) for g in range(GROUPS)]
                 for g in range(GROUPS):
                     quantise(j + 1, g, halves[g])
-            store_plain(j, THETA, multiply(j, THETA))
+            store_plain(j, THETA, first_two[THETA] if j == 0 else multiply(j, THETA))
             store_pooled(j, PHI, multiply(j, PHI))

@@ -167,12 +167,11 @@ def tile_nonlocalblocknd_pa_kernel(
                 stop=(g == GROUPS - 1),
             )
 
-        def multiply(j, c):
-            banks = four_banks()
-            for d in range(D_TILES):
-                for g in range(GROUPS):
-                    one_pass(j, c, d, g, banks[d])
-            return banks
+        def multiply(j, c, d):
+            bank = psum.tile([P, CHUNK], F32, name="acc", tag="acc")
+            for g in range(GROUPS):
+                one_pass(j, c, d, g, bank)
+            return bank
 
         def multiply_first_two():
             banks = {G: four_banks(), THETA: four_banks()}
@@ -182,41 +181,45 @@ def tile_nonlocalblocknd_pa_kernel(
                         one_pass(0, c, d, g, banks[c][d])
             return banks
 
-        def store_plain(j, c, banks):
-            for d in range(D_TILES):
-                plain = results.tile([P, CHUNK], F32, name="plain")
-                nc.scalar.activation(
-                    out=plain[:],
-                    in_=banks[d][:],
-                    func=mybir.ActivationFunctionType.Identity,
-                    bias=bias_of(c, d),
-                )
-                nc.sync.dma_start(
-                    out=dram_out[c][:, d, j * CHUNK : (j + 1) * CHUNK], in_=plain[:]
-                )
+        def store_plain(j, c, d, bank):
+            plain = results.tile([P, CHUNK], F32, name="plain")
+            nc.scalar.activation(
+                out=plain[:],
+                in_=bank[:],
+                func=mybir.ActivationFunctionType.Identity,
+                bias=bias_of(c, d),
+            )
+            nc.sync.dma_start(
+                out=dram_out[c][:, d, j * CHUNK : (j + 1) * CHUNK], in_=plain[:]
+            )
 
-        def store_pooled(j, c, banks):
-            for d in range(D_TILES):
-                pooled = results.tile([P, POOLED], F32, name="pooled")
-                nc.vector.tensor_reduce(
-                    out=pooled[:].rearrange("p (a w) -> p a w", w=WIDTH // WINDOW),
-                    in_=banks[d][:].rearrange(
-                        "p (a u w v) -> p a w u v", u=WINDOW, w=WIDTH // WINDOW, v=WINDOW
-                    ),
-                    axis=mybir.AxisListType.XY,
-                    op=mybir.AluOpType.max,
-                )
-                nc.gpsimd.tensor_scalar(
-                    out=pooled[:],
-                    in0=pooled[:],
-                    scalar1=1.0,
-                    scalar2=bias_of(c, d),
-                    op0=mybir.AluOpType.mult,
-                    op1=mybir.AluOpType.add,
-                )
-                nc.sync.dma_start(
-                    out=dram_out[c][:, d, j * POOLED : (j + 1) * POOLED], in_=pooled[:]
-                )
+        def store_pooled(j, c, d, bank):
+            pooled = results.tile([P, POOLED], F32, name="pooled")
+            nc.vector.tensor_reduce(
+                out=pooled[:].rearrange("p (a w) -> p a w", w=WIDTH // WINDOW),
+                in_=bank[:].rearrange(
+                    "p (a u w v) -> p a w u v", u=WINDOW, w=WIDTH // WINDOW, v=WINDOW
+                ),
+                axis=mybir.AxisListType.XY,
+                op=mybir.AluOpType.max,
+            )
+            nc.gpsimd.tensor_scalar(
+                out=pooled[:],
+                in0=pooled[:],
+                scalar1=1.0,
+                scalar2=bias_of(c, d),
+                op0=mybir.AluOpType.mult,
+                op1=mybir.AluOpType.add,
+            )
+            nc.sync.dma_start(
+                out=dram_out[c][:, d, j * POOLED : (j + 1) * POOLED], in_=pooled[:]
+            )
+
+        def store(j, c, d, bank):
+            if c == THETA:
+                store_plain(j, c, d, bank)
+            else:
+                store_pooled(j, c, d, bank)
 
         def idle_matmul(operand):
             unused = psum.tile([P, CHUNK], F32, name="unused", tag="acc")
@@ -230,12 +233,24 @@ def tile_nonlocalblocknd_pa_kernel(
         for g in range(GROUPS):
             quantise(0, g, regroup(0, g, HEAD_VECTOR_COLS))
 
-        for j in range(CHUNKS):
-            first_two = multiply_first_two() if j == 0 else {}
-            store_pooled(j, G, first_two[G] if j == 0 else multiply(j, G))
-            if j + 1 < CHUNKS:
-                halves = [regroup(j + 1, g, STEADY_VECTOR_COLS) for g in range(GROUPS)]
-                for g in range(GROUPS):
-                    quantise(j + 1, g, halves[g])
-            store_plain(j, THETA, first_two[THETA] if j == 0 else multiply(j, THETA))
-            store_pooled(j, PHI, multiply(j, PHI))
+        first_two = multiply_first_two()
+        for d in range(D_TILES):
+            store(0, G, d, first_two[G][d])
+        halves = [regroup(1, g, STEADY_VECTOR_COLS) for g in range(GROUPS)]
+        for g in range(GROUPS):
+            quantise(1, g, halves[g])
+        for d in range(D_TILES):
+            store(0, THETA, d, first_two[THETA][d])
+        for d in range(D_TILES):
+            store(0, PHI, d, multiply(0, PHI, d))
+
+        for j in range(1, CHUNKS):
+            more = j + 1 < CHUNKS
+            halves = []
+            for d in range(D_TILES):
+                for c in (THETA, G, PHI):
+                    store(j, c, d, multiply(j, c, d))
+                if more and d > 0 and d - 1 < GROUPS:
+                    quantise(j + 1, d - 1, halves[d - 1])
+                if more and d < GROUPS:
+                    halves.append(regroup(j + 1, d, STEADY_VECTOR_COLS))

@@ -24,6 +24,8 @@ POSITIONS = FRAMES * HEIGHT * WIDTH
 CHUNK = 512
 CHUNKS = POSITIONS // CHUNK
 WINDOW = 2
+HALF = CHUNK // 2
+NARROW = 128
 POOLED = CHUNK // (WINDOW * WINDOW)
 PSUM_BANKS = 8
 RESULT_BUFS = 16
@@ -94,6 +96,7 @@ def tile_nonlocalblocknd_pa_kernel(
         for c in range(CONVS):
             bias_words.append(keep.tile([P, D_TILES, 2], BF16, name="bias_words_%d" % c))
         zeros = keep.tile([P, CHUNK], BF16, name="zeros")
+        landed = keep.tile([P, 2], BF16, name="landed")
 
         def load_x(j, g):
             nc.sync.dma_start(
@@ -116,13 +119,6 @@ def tile_nonlocalblocknd_pa_kernel(
         for c in (THETA, PHI):
             nc.vector.memset(w_scales[c][:].rearrange("p g n -> p (g n)").bitcast(I32), 0)
 
-        with nc.allow_non_contiguous_dma(reason="one bias value to a partition"):
-            for c in range(CONVS):
-                nc.gpsimd.dma_start(
-                    out=bias_words[c][:, :, 0:1],
-                    in_=dram_bias[c].rearrange("(d p o) -> p d o", p=P, o=1),
-                )
-
         def bias_of(c, d):
             return bias_words[c][:, d, 0:1]
 
@@ -136,6 +132,14 @@ def tile_nonlocalblocknd_pa_kernel(
         for j in range(2, CHUNKS):
             for g in range(GROUPS):
                 load_x(j, g)
+
+        nc.gpsimd.tensor_copy(out=landed[:], in_=raw[(0, 1)][:, 0, 0:2])
+        with nc.allow_non_contiguous_dma(reason="one bias value to a partition"):
+            for c in (THETA, G, PHI):
+                nc.gpsimd.dma_start(
+                    out=bias_words[c][:, :, 0:1],
+                    in_=dram_bias[c].rearrange("(d p o) -> p d o", p=P, o=1),
+                )
 
         def regroup(j, g, vector_cols):
             grouped = stage.tile([P, CHUNK, PACK], BF16, name="grouped", align_bytes=64)
@@ -193,7 +197,7 @@ def tile_nonlocalblocknd_pa_kernel(
                 out=dram_out[c][:, d, j * CHUNK : (j + 1) * CHUNK], in_=plain[:]
             )
 
-        def store_pooled(j, c, d, bank):
+        def pool(bank):
             pooled = results.tile([P, POOLED], F32, name="pooled")
             nc.vector.tensor_reduce(
                 out=pooled[:].rearrange("p (a w) -> p a w", w=WIDTH // WINDOW),
@@ -203,6 +207,10 @@ def tile_nonlocalblocknd_pa_kernel(
                 axis=mybir.AxisListType.XY,
                 op=mybir.AluOpType.max,
             )
+            return pooled
+
+        def store_pooled(j, c, d, bank):
+            pooled = pool(bank)
             nc.gpsimd.tensor_scalar(
                 out=pooled[:],
                 in0=pooled[:],
@@ -214,6 +222,46 @@ def tile_nonlocalblocknd_pa_kernel(
             nc.sync.dma_start(
                 out=dram_out[c][:, d, j * POOLED : (j + 1) * POOLED], in_=pooled[:]
             )
+
+        def multiply_half(part):
+            bank = psum.tile([P, HALF], F32, name="half", tag="acc")
+            j, d = CHUNKS - 1, D_TILES - 1
+            for q in range(HALF // NARROW):
+                first = part * HALF + q * NARROW
+                cols = slice(first, first + NARROW)
+                for g in range(GROUPS):
+                    nc.tensor.matmul_mx(
+                        out=bank[:, q * NARROW : (q + 1) * NARROW],
+                        lhsT=w_words[THETA][:, g, 2 * P * d : 2 * P * (d + 1)].bitcast(FP4X4),
+                        lhsT_scale=w_scales[THETA][:, g, P * d : P * (d + 1)],
+                        rhs=x_codes[(j, g)][:, cols].bitcast(FP8X4),
+                        rhs_scale=x_scales[(j, g)][:, cols],
+                        start=(g == 0),
+                        stop=(g == GROUPS - 1),
+                    )
+            return bank
+
+        def store_half(part, bank):
+            j, d = CHUNKS - 1, D_TILES - 1
+            half = results.tile([P, HALF], F32, name="half_out")
+            if part == 0:
+                nc.scalar.activation(
+                    out=half[:],
+                    in_=bank[:],
+                    func=mybir.ActivationFunctionType.Identity,
+                    bias=bias_of(THETA, d),
+                )
+            else:
+                nc.vector.tensor_scalar(
+                    out=half[:],
+                    in0=bank[:],
+                    scalar1=1.0,
+                    scalar2=bias_of(THETA, d),
+                    op0=mybir.AluOpType.mult,
+                    op1=mybir.AluOpType.add,
+                )
+            first = j * CHUNK + part * HALF
+            nc.sync.dma_start(out=dram_out[THETA][:, d, first : first + HALF], in_=half[:])
 
         def store(j, c, d, bank):
             if c == THETA:
@@ -244,13 +292,29 @@ def tile_nonlocalblocknd_pa_kernel(
         for d in range(D_TILES):
             store(0, PHI, d, multiply(0, PHI, d))
 
-        for j in range(1, CHUNKS):
-            more = j + 1 < CHUNKS
-            halves = []
+        for j in range(1, CHUNKS - 1):
             for d in range(D_TILES):
-                for c in (THETA, G, PHI):
+                store(j, G, d, multiply(j, G, d))
+            halves = [regroup(j + 1, g, STEADY_VECTOR_COLS) for g in range(GROUPS)]
+            for g in range(GROUPS):
+                quantise(j + 1, g, halves[g])
+            for c in (THETA, PHI):
+                for d in range(D_TILES):
                     store(j, c, d, multiply(j, c, d))
-                if more and d > 0 and d - 1 < GROUPS:
-                    quantise(j + 1, d - 1, halves[d - 1])
-                if more and d < GROUPS:
-                    halves.append(regroup(j + 1, d, STEADY_VECTOR_COLS))
+
+        last = CHUNKS - 1
+        for c, tiles in ((G, D_TILES), (THETA, D_TILES - 1), (PHI, D_TILES - 1)):
+            for d in range(tiles):
+                store(last, c, d, multiply(last, c, d))
+        pooled = pool(multiply(last, PHI, D_TILES - 1))
+        store_half(0, multiply_half(0))
+        nc.scalar.activation(
+            out=pooled[:],
+            in_=pooled[:],
+            func=mybir.ActivationFunctionType.Identity,
+            bias=bias_of(PHI, D_TILES - 1),
+        )
+        nc.sync.dma_start(
+            out=dram_out[PHI][:, D_TILES - 1, last * POOLED : CHUNKS * POOLED], in_=pooled[:]
+        )
+        store_half(1, multiply_half(1))

@@ -143,18 +143,23 @@ def tile_nonlocalblocknd_pa_kernel(
 
         def regroup(j, g, vector_cols):
             grouped = stage.tile([P, CHUNK, PACK], BF16, name="grouped", align_bytes=64)
-            src = raw[(j, g)][:].rearrange("p t (n i) -> p n t i", i=RUN)
-            dst = grouped[:].rearrange("p (n i) t -> p n t i", i=RUN)
-            split = (CHUNK - vector_cols) // RUN
-            nc.scalar.copy(out=dst[:, :split], in_=src[:, :split])
-            nc.vector.tensor_copy(out=dst[:, split:], in_=src[:, split:])
+            regroup_part(j, g, grouped, 0, CHUNK, vector_cols)
             return grouped
 
-        def quantise(j, g, grouped):
+        def regroup_part(j, g, grouped, begin, end, vector_cols):
+            src = raw[(j, g)][:].rearrange("p t (n i) -> p n t i", i=RUN)
+            dst = grouped[:].rearrange("p (n i) t -> p n t i", i=RUN)
+            split = (end - vector_cols) // RUN
+            scalar_part = slice(begin // RUN, split)
+            vector_part = slice(split, end // RUN)
+            nc.scalar.copy(out=dst[:, scalar_part], in_=src[:, scalar_part])
+            nc.vector.tensor_copy(out=dst[:, vector_part], in_=src[:, vector_part])
+
+        def quantise(j, g, grouped, begin=0, end=CHUNK):
             nc.vector.quantize_mx(
-                out=x_codes[(j, g)][:].bitcast(FP8X4),
-                scales=x_scales[(j, g)][:],
-                in_=grouped[:].rearrange("p n t -> p (n t)"),
+                out=x_codes[(j, g)][:, begin:end].bitcast(FP8X4),
+                scales=x_scales[(j, g)][:, begin:end],
+                in_=grouped[:, begin:end, :].rearrange("p n t -> p (n t)"),
             )
 
         def four_banks():
@@ -279,7 +284,11 @@ def tile_nonlocalblocknd_pa_kernel(
             idle_matmul(raw[(0, 0)][:, 0, :])
 
         for g in range(GROUPS):
-            quantise(0, g, regroup(0, g, HEAD_VECTOR_COLS))
+            grouped = stage.tile([P, CHUNK, PACK], BF16, name="grouped", align_bytes=64)
+            for begin in range(0, CHUNK, HALF):
+                regroup_part(0, g, grouped, begin, begin + HALF, HEAD_VECTOR_COLS // 2)
+            for begin in range(0, CHUNK, HALF):
+                quantise(0, g, grouped, begin, begin + HALF)
 
         first_two = multiply_first_two()
         for d in range(D_TILES):

@@ -37,6 +37,7 @@ PHI = 2
 CONVS = 3
 
 HEAD_VECTOR_COLS = 352
+EARLY_VECTOR_COLS = 256
 STEADY_VECTOR_COLS = 128
 
 WARM_ZEROS = 5
@@ -127,15 +128,16 @@ def tile_nonlocalblocknd_pa_kernel(
         load_x(0, 1)
         load_weight(THETA)
         load_x(1, 0)
-        load_x(1, 1)
         load_weight(PHI)
+        load_x(1, 1)
         for j in range(2, CHUNKS):
             for g in range(GROUPS):
                 load_x(j, g)
 
-        nc.gpsimd.tensor_copy(out=landed[:], in_=raw[(0, 1)][:, 0, 0:2])
         with nc.allow_non_contiguous_dma(reason="one bias value to a partition"):
             for c in (THETA, G, PHI):
+                if c == G:
+                    nc.gpsimd.tensor_copy(out=landed[:], in_=raw[(0, 1)][:, 0, 0:2])
                 nc.gpsimd.dma_start(
                     out=bias_words[c][:, :, 0:1],
                     in_=dram_bias[c].rearrange("(d p o) -> p d o", p=P, o=1),
@@ -162,9 +164,6 @@ def tile_nonlocalblocknd_pa_kernel(
                 in_=grouped[:, begin:end, :].rearrange("p n t -> p (n t)"),
             )
 
-        def four_banks():
-            return [psum.tile([P, CHUNK], F32, name="acc", tag="acc") for d in range(D_TILES)]
-
         def one_pass(j, c, d, g, bank):
             nc.tensor.matmul_mx(
                 out=bank[:],
@@ -183,11 +182,15 @@ def tile_nonlocalblocknd_pa_kernel(
             return bank
 
         def multiply_first_two():
-            banks = {G: four_banks(), THETA: four_banks()}
-            for g in range(GROUPS):
-                for c in (G, THETA):
-                    for d in range(D_TILES):
-                        one_pass(0, c, d, g, banks[c][d])
+            tiles = [(c, d) for d in range(D_TILES) for c in (G, THETA)]
+            banks = {}
+            for tile in tiles:
+                banks[tile] = psum.tile([P, CHUNK], F32, name="acc", tag="acc")
+            for c in (G, THETA):
+                for d in range(D_TILES):
+                    one_pass(0, c, d, 0, banks[(c, d)])
+            for c, d in tiles:
+                one_pass(0, c, d, 1, banks[(c, d)])
             return banks
 
         def store_plain(j, c, d, bank):
@@ -291,13 +294,16 @@ def tile_nonlocalblocknd_pa_kernel(
                 quantise(0, g, grouped, begin, begin + HALF)
 
         first_two = multiply_first_two()
-        for d in range(D_TILES):
-            store(0, G, d, first_two[G][d])
-        halves = [regroup(1, g, STEADY_VECTOR_COLS) for g in range(GROUPS)]
-        for g in range(GROUPS):
-            quantise(1, g, halves[g])
-        for d in range(D_TILES):
-            store(0, THETA, d, first_two[THETA][d])
+        half = regroup(1, 0, EARLY_VECTOR_COLS)
+        for c, d in ((G, 0), (THETA, 0), (G, 1)):
+            store(0, c, d, first_two[(c, d)])
+        quantise(1, 0, half)
+        half = regroup(1, 1, EARLY_VECTOR_COLS)
+        for c, d in ((THETA, 1), (G, 2), (THETA, 2)):
+            store(0, c, d, first_two[(c, d)])
+        quantise(1, 1, half)
+        for c, d in ((G, 3), (THETA, 3)):
+            store(0, c, d, first_two[(c, d)])
         for d in range(D_TILES):
             store(0, PHI, d, multiply(0, PHI, d))
 

@@ -307,20 +307,18 @@ def tile_nonlocalblocknd_pa_kernel(
         for d in range(D_TILES):
             store(0, PHI, d, multiply(0, PHI, d))
 
-        for j in range(1, CHUNKS - 1):
-            for d in range(D_TILES):
-                store(j, G, d, multiply(j, G, d))
-            halves = [regroup(j + 1, g, STEADY_VECTOR_COLS) for g in range(GROUPS)]
-            for g in range(GROUPS):
-                quantise(j + 1, g, halves[g])
-            for c in (THETA, PHI):
-                for d in range(D_TILES):
-                    store(j, c, d, multiply(j, c, d))
-
         last = CHUNKS - 1
-        for c, tiles in ((G, D_TILES), (THETA, D_TILES - 1), (PHI, D_TILES - 1)):
-            for d in range(tiles):
-                store(last, c, d, multiply(last, c, d))
+        for j in range(1, CHUNKS):
+            for d in range(D_TILES):
+                if j < last and d < GROUPS:
+                    half = regroup(j + 1, d, STEADY_VECTOR_COLS)
+                if j < last or d < D_TILES - 1:
+                    for c in (THETA, G, PHI):
+                        store(j, c, d, multiply(j, c, d))
+                if j < last and d < GROUPS:
+                    quantise(j + 1, d, half)
+
+        store(last, G, D_TILES - 1, multiply(last, G, D_TILES - 1))
         pooled = pool(multiply(last, PHI, D_TILES - 1))
         store_half(0, multiply_half(0))
         nc.scalar.activation(

from contextlib import ExitStack

import concourse.mybir as mybir

F32 = mybir.dt.float32
BF16 = mybir.dt.bfloat16
I32 = mybir.dt.int32
U32 = mybir.dt.uint32
U8 = mybir.dt.uint8
FP8X4 = mybir.dt.float8_e4m3fn_x4
FP4X4 = mybir.dt.float4_e2m1fn_x4

P = 128
PACK = 4
K_PASS = P * PACK
CHANNELS = 1024
GROUPS = CHANNELS // K_PASS
D = 512
D_TILES = D // P
FRAMES = 8
HEIGHT = 16
WIDTH = 16
POSITIONS = FRAMES * HEIGHT * WIDTH
CHUNK = 512
CHUNKS = POSITIONS // CHUNK
WINDOW = 2
HALF = CHUNK // 2
NARROW = 128
POOLED = CHUNK // (WINDOW * WINDOW)
PSUM_BANKS = 8
RESULT_BUFS = 16
RUN = 4

G = 0
THETA = 1
PHI = 2
CONVS = 3

HEAD_VECTOR_COLS = 352
EARLY_VECTOR_COLS = 256
STEADY_VECTOR_COLS = 128

WARM_ZEROS = 5
WARM_RAW = 3

FLOPS = 2 * CONVS * D * CHANNELS * POSITIONS


def tile_nonlocalblocknd_pa_kernel(
    tc,
    x,
    g_w_words,
    g_w_scales,
    g_b,
    theta_w_words,
    theta_w_scales,
    theta_b,
    phi_w_words,
    phi_w_scales,
    phi_b,
    out_0,
    out_1,
    out_2,
):
    nc = tc.nc
    dram_words = (g_w_words, theta_w_words, phi_w_words)
    dram_scales = (g_w_scales, theta_w_scales, phi_w_scales)
    dram_bias = (g_b, theta_b, phi_b)
    dram_out = [o[0].rearrange("(d p) n -> p d n", p=P) for o in (out_0, out_1, out_2)]
    x_rows = x[0].rearrange("(g p t) f h w -> g p t (f h w)", g=GROUPS, p=P, t=PACK)

    with ExitStack() as ctx:
        keep = ctx.enter_context(tc.tile_pool(name="keep", bufs=1))
        stage = ctx.enter_context(tc.tile_pool(name="stage", bufs=4))
        results = ctx.enter_context(tc.tile_pool(name="results", bufs=RESULT_BUFS))
        psum = ctx.enter_context(tc.psum_pool(name="psum", bufs=PSUM_BANKS))
        ctx.enter_context(tc.manual_schedule())

        raw = {}
        x_codes = {}
        x_scales = {}
        for j in range(CHUNKS):
            for g in range(GROUPS):
                raw[(j, g)] = keep.tile([P, PACK, CHUNK], BF16, name="raw_%d_%d" % (j, g))
                x_codes[(j, g)] = keep.tile(
                    [P, CHUNK], U32, name="x_codes_%d_%d" % (j, g), align_bytes=64
                )
                x_scales[(j, g)] = keep.tile(
                    [P, CHUNK], U8, name="x_scales_%d_%d" % (j, g), align_bytes=64
                )
        w_words = []
        w_scales = []
        for c in range(CONVS):
            w_words.append(keep.tile([P, GROUPS, 2 * D], U8, name="w_words_%d" % c, align_bytes=64))
            w_scales.append(keep.tile([P, GROUPS, D], U8, name="w_scales_%d" % c, align_bytes=64))
        bias_words = []
        for c in range(CONVS):
            bias_words.append(keep.tile([P, D_TILES, 2], BF16, name="bias_words_%d" % c))
        zeros = keep.tile([P, CHUNK], BF16, name="zeros")
        landed = keep.tile([P, 2], BF16, name="landed")

        def load_x(j, g):
            nc.sync.dma_start(
                out=raw[(j, g)][:], in_=x_rows[g, :, :, j * CHUNK : (j + 1) * CHUNK]
            )

        def load_weight(c):
            for r in range(4):
                nc.sync.dma_start(
                    out=w_scales[c][r:P:32, :, :].bitcast(I32),
                    in_=dram_scales[c][:, r:16:4, :].rearrange("g q n -> q g n").bitcast(I32),
                )
            nc.sync.dma_start(
                out=w_words[c][:].bitcast(I32),
                in_=dram_words[c].rearrange("g p b -> p g b").bitcast(I32),
            )

        nc.vector.memset(w_scales[G][:].rearrange("p g n -> p (g n)").bitcast(I32), 0)
        nc.vector.memset(zeros[:], 0.0)
        for c in (THETA, PHI):
            nc.vector.memset(w_scales[c][:].rearrange("p g n -> p (g n)").bitcast(I32), 0)

        def bias_of(c, d):
            return bias_words[c][:, d, 0:1]

        load_x(0, 0)
        load_weight(G)
        load_x(0, 1)
        load_weight(THETA)
        load_x(1, 0)
        load_weight(PHI)
        load_x(1, 1)
        for j in range(2, CHUNKS):
            for g in range(GROUPS):
                load_x(j, g)

        with nc.allow_non_contiguous_dma(reason="one bias value to a partition"):
            for c in (THETA, G, PHI):
                if c == G:
                    nc.gpsimd.tensor_copy(out=landed[:], in_=raw[(0, 1)][:, 0, 0:2])
                nc.gpsimd.dma_start(
                    out=bias_words[c][:, :, 0:1],
                    in_=dram_bias[c].rearrange("(d p o) -> p d o", p=P, o=1),
                )

        def regroup(j, g, vector_cols):
            grouped = stage.tile([P, CHUNK, PACK], BF16, name="grouped", align_bytes=64)
            regroup_part(j, g, grouped, 0, CHUNK, vector_cols)
            return grouped

        def regroup_part(j, g, grouped, begin, end, vector_cols):
            src = raw[(j, g)][:].rearrange("p t (n i) -> p n t i", i=RUN)
            dst = grouped[:].rearrange("p (n i) t -> p n t i", i=RUN)
            split = (end - vector_cols) // RUN
            scalar_part = slice(begin // RUN, split)
            vector_part = slice(split, end // RUN)
            nc.scalar.copy(out=dst[:, scalar_part], in_=src[:, scalar_part])
            nc.vector.tensor_copy(out=dst[:, vector_part], in_=src[:, vector_part])

        def quantise(j, g, grouped, begin=0, end=CHUNK):
            nc.vector.quantize_mx(
                out=x_codes[(j, g)][:, begin:end].bitcast(FP8X4),
                scales=x_scales[(j, g)][:, begin:end],
                in_=grouped[:, begin:end, :].rearrange("p n t -> p (n t)"),
            )

        def one_pass(j, c, d, g, bank):
            nc.tensor.matmul_mx(
                out=bank[:],
                lhsT=w_words[c][:, g, 2 * P * d : 2 * P * (d + 1)].bitcast(FP4X4),
                lhsT_scale=w_scales[c][:, g, P * d : P * (d + 1)],
                rhs=x_codes[(j, g)][:].bitcast(FP8X4),
                rhs_scale=x_scales[(j, g)][:],
                start=(g == 0),
                stop=(g == GROUPS - 1),
            )

        def multiply(j, c, d):
            bank = psum.tile([P, CHUNK], F32, name="acc", tag="acc")
            for g in range(GROUPS):
                one_pass(j, c, d, g, bank)
            return bank

        def multiply_first_two():
            tiles = [(c, d) for d in range(D_TILES) for c in (G, THETA)]
            banks = {}
            for tile in tiles:
                banks[tile] = psum.tile([P, CHUNK], F32, name="acc", tag="acc")
            for c in (G, THETA):
                for d in range(D_TILES):
                    one_pass(0, c, d, 0, banks[(c, d)])
            for c, d in tiles:
                one_pass(0, c, d, 1, banks[(c, d)])
            return banks

        def store_plain(j, c, d, bank):
            plain = results.tile([P, CHUNK], F32, name="plain")
            nc.scalar.activation(
                out=plain[:],
                in_=bank[:],
                func=mybir.ActivationFunctionType.Identity,
                bias=bias_of(c, d),
            )
            nc.sync.dma_start(
                out=dram_out[c][:, d, j * CHUNK : (j + 1) * CHUNK], in_=plain[:]
            )

        def pool(bank):
            pooled = results.tile([P, POOLED], F32, name="pooled")
            nc.vector.tensor_reduce(
                out=pooled[:].rearrange("p (a w) -> p a w", w=WIDTH // WINDOW),
                in_=bank[:].rearrange(
                    "p (a u w v) -> p a w u v", u=WINDOW, w=WIDTH // WINDOW, v=WINDOW
                ),
                axis=mybir.AxisListType.XY,
                op=mybir.AluOpType.max,
            )
            return pooled

        def store_pooled(j, c, d, bank):
            pooled = pool(bank)
            nc.gpsimd.tensor_scalar(
                out=pooled[:],
                in0=pooled[:],
                scalar1=1.0,
                scalar2=bias_of(c, d),
                op0=mybir.AluOpType.mult,
                op1=mybir.AluOpType.add,
            )
            nc.sync.dma_start(
                out=dram_out[c][:, d, j * POOLED : (j + 1) * POOLED], in_=pooled[:]
            )

        def multiply_half(part):
            bank = psum.tile([P, HALF], F32, name="half", tag="acc")
            j, d = CHUNKS - 1, D_TILES - 1
            for q in range(HALF // NARROW):
                first = part * HALF + q * NARROW
                cols = slice(first, first + NARROW)
                for g in range(GROUPS):
                    nc.tensor.matmul_mx(
                        out=bank[:, q * NARROW : (q + 1) * NARROW],
                        lhsT=w_words[THETA][:, g, 2 * P * d : 2 * P * (d + 1)].bitcast(FP4X4),
                        lhsT_scale=w_scales[THETA][:, g, P * d : P * (d + 1)],
                        rhs=x_codes[(j, g)][:, cols].bitcast(FP8X4),
                        rhs_scale=x_scales[(j, g)][:, cols],
                        start=(g == 0),
                        stop=(g == GROUPS - 1),
                    )
            return bank

        def store_half(part, bank):
            j, d = CHUNKS - 1, D_TILES - 1
            half = results.tile([P, HALF], F32, name="half_out")
            if part == 0:
                nc.scalar.activation(
                    out=half[:],
                    in_=bank[:],
                    func=mybir.ActivationFunctionType.Identity,
                    bias=bias_of(THETA, d),
                )
            else:
                nc.vector.tensor_scalar(
                    out=half[:],
                    in0=bank[:],
                    scalar1=1.0,
                    scalar2=bias_of(THETA, d),
                    op0=mybir.AluOpType.mult,
                    op1=mybir.AluOpType.add,
                )
            first = j * CHUNK + part * HALF
            nc.sync.dma_start(out=dram_out[THETA][:, d, first : first + HALF], in_=half[:])

        def store(j, c, d, bank):
            if c == THETA:
                store_plain(j, c, d, bank)
            else:
                store_pooled(j, c, d, bank)

        def idle_matmul(operand):
            unused = psum.tile([P, CHUNK], F32, name="unused", tag="acc")
            nc.tensor.matmul(unused[:], lhsT=operand[:, :P], rhs=operand, start=True, stop=True)

        for i in range(WARM_ZEROS):
            idle_matmul(zeros[:])
        for i in range(WARM_RAW):
            idle_matmul(raw[(0, 0)][:, 0, :])

        for g in range(GROUPS):
            grouped = stage.tile([P, CHUNK, PACK], BF16, name="grouped", align_bytes=64)
            for begin in range(0, CHUNK, HALF):
                regroup_part(0, g, grouped, begin, begin + HALF, HEAD_VECTOR_COLS // 2)
            for begin in range(0, CHUNK, HALF):
                quantise(0, g, grouped, begin, begin + HALF)

        first_two = multiply_first_two()
        half = regroup(1, 0, EARLY_VECTOR_COLS)
        for c, d in ((G, 0), (THETA, 0), (G, 1)):
            store(0, c, d, first_two[(c, d)])
        quantise(1, 0, half)
        half = regroup(1, 1, EARLY_VECTOR_COLS)
        for c, d in ((THETA, 1), (G, 2), (THETA, 2)):
            store(0, c, d, first_two[(c, d)])
        quantise(1, 1, half)
        for c, d in ((G, 3), (THETA, 3)):
            store(0, c, d, first_two[(c, d)])
        for d in range(D_TILES):
            store(0, PHI, d, multiply(0, PHI, d))

        last = CHUNKS - 1
        for j in range(1, CHUNKS):
            for d in range(D_TILES):
                if j < last and d < GROUPS:
                    half = regroup(j + 1, d, STEADY_VECTOR_COLS)
                if j < last or d < D_TILES - 1:
                    for c in (THETA, G, PHI):
                        store(j, c, d, multiply(j, c, d))
                if j < last and d < GROUPS:
                    quantise(j + 1, d, half)

        store(last, G, D_TILES - 1, multiply(last, G, D_TILES - 1))
        pooled = pool(multiply(last, PHI, D_TILES - 1))
        store_half(0, multiply_half(0))
        nc.scalar.activation(
            out=pooled[:],
            in_=pooled[:],
            func=mybir.ActivationFunctionType.Identity,
            bias=bias_of(PHI, D_TILES - 1),
        )
        nc.sync.dma_start(
            out=dram_out[PHI][:, D_TILES - 1, last * POOLED : CHUNKS * POOLED], in_=pooled[:]
        )
        store_half(1, multiply_half(1))
